import numpy as np
import ml_dtypes


def mxq(x, axis, fmt="e4m3"):
    dtype, down = {"e4m3": (ml_dtypes.float8_e4m3fn, 7), "e5m2": (ml_dtypes.float8_e5m2, 14)}[fmt]
    v = np.moveaxis(np.asarray(x, np.float32).astype(ml_dtypes.bfloat16).astype(np.float64), axis, -1)
    blocks = v.reshape(v.shape[:-1] + (-1, 32))
    amax = np.abs(blocks).max(-1, keepdims=True)
    byte = np.maximum(np.where(amax > 0, np.frexp(amax)[1] - 1 + 127, 0) - down, 1)
    scale = np.exp2(byte - 127.0)
    codes = (blocks / scale).astype(np.float32).astype(dtype).astype(np.float64)
    return np.moveaxis((codes * scale).reshape(v.shape), -1, axis)


WIDE = False


def mx_kscale(k):
    if not WIDE:
        return np.ones(k)
    levels = np.array([10, -10, 5, -5, 0])
    a = np.random.permutation(np.resize(levels, k // 512 * 4)).reshape(k // 512, 4)
    idx = np.arange(k)
    return np.exp2(a[idx // 512, idx % 128 // 32])


BF16 = ml_dtypes.bfloat16


def bf(x):
    return np.asarray(x, np.float32).astype(BF16)


def f64(x):
    return np.asarray(x).astype(np.float64)


E2M1 = np.array([0.0, 0.5, 1.0, 1.5, 2.0, 3.0, 4.0, 6.0, -0.0, -0.5, -1.0, -1.5, -2.0, -3.0, -4.0, -6.0])


def pack_weight(w, fmt):
    k, n = w.shape
    w = f64(bf(w)).reshape(k // 32, 32, n)
    amax = np.abs(w).max(1)
    if fmt == "e4m3":
        byte = np.frexp(amax)[1] - 1 + 127 - 7
    else:
        mant, ex = np.frexp(amax / 6.0)
        byte = np.where(mant > 0.5, ex, ex - 1) + 127
    byte = np.clip(np.where(amax > 0, byte, 1), 1, 254)
    scaled = (w * np.exp2(127.0 - byte)[:, None, :]).reshape(k, n).astype(np.float32)
    by_word = np.ascontiguousarray(scaled.reshape(k // 512, 128, 4, n).transpose(0, 1, 3, 2))
    if fmt == "e4m3":
        words = by_word.astype(ml_dtypes.float8_e4m3fn).view(np.uint8)
    else:
        c = by_word.astype(ml_dtypes.float4_e2m1fn).view(np.uint8) & 0xF
        words = c[..., 0::2] | (c[..., 1::2] << 4)
    return np.ascontiguousarray(words), np.ascontiguousarray(byte.astype(np.uint8).reshape(k // 512, 16, n))


def unpack_weight(words, scales, fmt):
    g, p, n, _ = words.shape
    if fmt == "e4m3":
        vals = np.ascontiguousarray(words).view(ml_dtypes.float8_e4m3fn).astype(np.float64)
    else:
        nib = np.empty((g, p, n, 4), np.uint8)
        nib[..., 0::2] = words & 0xF
        nib[..., 1::2] = words >> 4
        vals = E2M1[nib]
    vals = vals * np.repeat(np.exp2(scales.astype(np.float64) - 127.0), 8, axis=1)[..., None]
    return vals.transpose(0, 1, 3, 2).reshape(g * 512, n)


B, N, F, FO, KC = 4, 512, 1024, 1024, 5


def setup_inputs():
    d = mx_kscale(N)
    d = d / d.max()
    a = np.random.standard_normal((N, N)) / np.sqrt(N)
    z0 = bf(np.random.standard_normal((B, N, F)) * d[:, None])
    z1 = bf(0.7 * np.random.standard_normal((B, N, F)) * d[:, None])
    lap = 0.5 * (a + a.T) * d[:, None] / d[None, :]
    words, scales = pack_weight(np.ascontiguousarray(lap.T), "e4m3")
    return {"z0": z0, "z1": z1, "L_words": words, "L_scales": scales}


def reference(z0, z1, L_words, L_scales):
    z0, z1 = f64(z0), f64(z1)
    lq = unpack_weight(L_words, L_scales, "e4m3").T
    z2 = 2.0 * (lq @ mxq(z1, 1, "e4m3")) - z0
    z3 = 2.0 * (lq @ mxq(z2, 1, "e4m3")) - z1
    return z2, z3

@@ -1,0 +1,170 @@
+from contextlib import ExitStack
+
+import concourse.mybir as mybir
+from concourse.masks import make_identity
+
+FP8X4 = mybir.dt.float8_e4m3fn_x4
+BF16 = mybir.dt.bfloat16
+F32 = mybir.dt.float32
+I32 = mybir.dt.int32
+U32 = mybir.dt.uint32
+U8 = mybir.dt.uint8
+MULT = mybir.AluOpType.mult
+SUBTRACT = mybir.AluOpType.subtract
+
+P = 128
+PACK = 4
+BATCH = 4
+NODES = P * PACK
+FEATURES = 1024
+TILE_F = 128
+RUN = 4
+GROUP_F = RUN * TILE_F
+GROUPS_PER_ITEM = FEATURES // GROUP_F
+GROUPS = BATCH * GROUPS_PER_ITEM
+VECTOR_REGROUPS = 2
+
+FLOPS = 2 * 2 * BATCH * NODES * NODES * FEATURES
+
+
+def tile_manualchebconv_pb_kernel(tc, z0, z1, L_words, L_scales, out_0, out_1):
+    nc = tc.nc
+
+    def by_group(dram):
+        rows = dram.rearrange("b (p t) f -> b p t f", t=PACK)
+        return [
+            rows[g // GROUPS_PER_ITEM][:, :, (g % GROUPS_PER_ITEM) * GROUP_F : (g % GROUPS_PER_ITEM + 1) * GROUP_F]
+            for g in range(GROUPS)
+        ]
+
+    z0_dram, z1_dram = by_group(z0), by_group(z1)
+    z2_dram, z3_dram = by_group(out_0), by_group(out_1)
+
+    with ExitStack() as ctx:
+        consts = ctx.enter_context(tc.tile_pool(name="consts", bufs=1))
+        inputs = ctx.enter_context(tc.tile_pool(name="inputs", bufs=1))
+        operands = ctx.enter_context(tc.tile_pool(name="operands", bufs=2))
+        sorted_pool = ctx.enter_context(tc.tile_pool(name="sorted", bufs=2 * RUN))
+        results = ctx.enter_context(tc.tile_pool(name="results", bufs=4))
+        product_banks = ctx.enter_context(tc.psum_pool(name="product_banks", bufs=RUN))
+        turned_banks = ctx.enter_context(tc.psum_pool(name="turned_banks", bufs=RUN))
+        ctx.enter_context(tc.manual_schedule())
+
+        identity = consts.tile([P, P], F32, name="identity")
+        make_identity(nc, identity[:])
+
+        l_words = consts.tile([P, NODES], U32, name="l_words", align_bytes=64)
+        l_scales = consts.tile([P, NODES], U8, name="l_scales", align_bytes=64)
+        nc.vector.memset(l_scales[:].bitcast(I32), 0)
+
+        z0_sb = [inputs.tile([P, PACK, GROUP_F], BF16, name="z0_sb%d" % g) for g in range(GROUPS)]
+        z1_sb = [inputs.tile([P, PACK, GROUP_F], BF16, name="z1_sb%d" % g) for g in range(GROUPS)]
+
+        nc.sync.dma_start(out=z1_sb[0][:], in_=z1_dram[0])
+        nc.sync.dma_start(out=l_words[:].bitcast(I32), in_=L_words[0].rearrange("p n t -> p (n t)").bitcast(I32))
+        for quadrant in range(4):
+            nc.sync.dma_start(
+                out=l_scales[32 * quadrant : 32 * quadrant + 4, :].bitcast(I32),
+                in_=L_scales[0, 4 * quadrant : 4 * quadrant + 4, :].bitcast(I32),
+            )
+        nc.sync.dma_start(out=z1_sb[1][:], in_=z1_dram[1])
+        for g in range(GROUPS):
+            nc.sync.dma_start(out=z0_sb[g][:], in_=z0_dram[g])
+            if g + 2 < GROUPS:
+                nc.sync.dma_start(out=z1_sb[g + 2][:], in_=z1_dram[g + 2])
+
+        grouped = {}
+        quantised = {}
+        sorted_products = {}
+        turned = {}
+        z2_sb = {}
+
+        def regroup(engine_copy, dst, src):
+            engine_copy(
+                out=dst[:].rearrange("p (c i) t -> p c t i", i=4),
+                in_=src[:].rearrange("p t (c i) -> p c t i", i=4),
+            )
+
+        def regroup_z1(g):
+            dst = operands.tile([P, GROUP_F, PACK], BF16, name="z1_grouped", align_bytes=64)
+            regroup(nc.vector.tensor_copy if g < VECTOR_REGROUPS else nc.scalar.copy, dst, z1_sb[g])
+            grouped[1, g] = dst
+
+        def regroup_z2(g):
+            dst = operands.tile([P, GROUP_F, PACK], BF16, name="z2_grouped", align_bytes=64)
+            regroup(nc.vector.tensor_copy, dst, z2_sb[g])
+            grouped[2, g] = dst
+
+        def quantise(step, g):
+            codes = operands.tile([P, GROUP_F], U32, name="codes%d" % step, align_bytes=64)
+            scales = operands.tile([P, GROUP_F], U8, name="scales%d" % step, align_bytes=64)
+            nc.vector.quantize_mx(
+                out=codes[:].bitcast(FP8X4),
+                scales=scales[:],
+                in_=grouped[step, g][:].rearrange("p f t -> p (f t)"),
+            )
+            quantised[step, g] = (codes, scales)
+
+        def multiply(step, g):
+            codes, scales = quantised[step, g]
+            sorted_products[step, g] = []
+            for u in range(RUN):
+                cols = slice(u * TILE_F, (u + 1) * TILE_F)
+                product = product_banks.tile([P, NODES], F32, name="product")
+                nc.tensor.matmul_mx(
+                    out=product[:],
+                    lhsT=codes[:, cols].bitcast(FP8X4),
+                    lhsT_scale=scales[:, cols],
+                    rhs=l_words[:].bitcast(FP8X4),
+                    rhs_scale=l_scales[:],
+                    start=True,
+                    stop=True,
+                )
+                by_t = sorted_pool.tile([P, PACK, P], F32, name="by_t")
+                nc.scalar.copy(out=by_t[:], in_=product[:].rearrange("f (p t) -> f t p", t=PACK))
+                sorted_products[step, g].append(by_t)
+
+        def turn(step, g):
+            turned[step, g] = []
+            for u in range(RUN):
+                bank = turned_banks.tile([P, PACK, TILE_F], F32, name="bank")
+                for t in range(PACK):
+                    nc.tensor.transpose(bank[:, t, :], sorted_products[step, g][u][:, t, :], identity[:])
+                turned[step, g].append(bank)
+
+        def combine(step, g, older, dram):
+            result = results.tile([P, PACK, GROUP_F], F32, name="result%d" % step)
+            for u in range(RUN):
+                cols = slice(u * TILE_F, (u + 1) * TILE_F)
+                nc.vector.scalar_tensor_tensor(
+                    out=result[:, :, cols],
+                    in0=turned[step, g][u][:],
+                    scalar=2.0,
+                    in1=older[g][:, :, cols],
+                    op0=MULT,
+                    op1=SUBTRACT,
+                )
+            nc.sync.dma_start(out=dram[g], in_=result[:])
+            return result
+
+        def first_combine(g):
+            z2_sb[g] = combine(1, g, z0_sb, z2_dram)
+
+        def second_combine(g):
+            combine(2, g, z1_sb, z3_dram)
+
+        def for_group(g, step_of_group, *args):
+            if 0 <= g < GROUPS:
+                step_of_group(*args, g)
+
+        for r in range(-3, GROUPS + 1):
+            for_group(r - 1, multiply, 2)
+            for_group(r + 1, multiply, 1)
+            for_group(r, first_combine)
+            for_group(r, regroup_z2)
+            for_group(r - 1, turn, 2)
+            for_group(r - 1, second_combine)
+            for_group(r + 1, turn, 1)
+            for_group(r, quantise, 2)
+            for_group(r + 2, quantise, 1)
+            for_group(r + 3, regroup_z1)

@@ -10,6 +10,7 @@ I32 = mybir.dt.int32
 U32 = mybir.dt.uint32
 U8 = mybir.dt.uint8
 MULT = mybir.AluOpType.mult
+ADD = mybir.AluOpType.add
 SUBTRACT = mybir.AluOpType.subtract
 
 P = 128
@@ -43,8 +44,9 @@ def tile_manualchebconv_pb_kernel(tc, z0, z1, L_words, L_scales, out_0, out_1):
     with ExitStack() as ctx:
         consts = ctx.enter_context(tc.tile_pool(name="consts", bufs=1))
         inputs = ctx.enter_context(tc.tile_pool(name="inputs", bufs=1))
+        regrouped_z1 = ctx.enter_context(tc.tile_pool(name="regrouped_z1", bufs=3))
         operands = ctx.enter_context(tc.tile_pool(name="operands", bufs=2))
-        sorted_pool = ctx.enter_context(tc.tile_pool(name="sorted", bufs=2 * RUN))
+        sorted_pool = ctx.enter_context(tc.tile_pool(name="sorted", bufs=3 * RUN))
         results = ctx.enter_context(tc.tile_pool(name="results", bufs=4))
         product_banks = ctx.enter_context(tc.psum_pool(name="product_banks", bufs=RUN))
         turned_banks = ctx.enter_context(tc.psum_pool(name="turned_banks", bufs=RUN))
@@ -81,18 +83,32 @@ def tile_manualchebconv_pb_kernel(tc, z0, z1, L_words, L_scales, out_0, out_1):
 
         def regroup(engine_copy, dst, src):
             engine_copy(
-                out=dst[:].rearrange("p (c i) t -> p c t i", i=4),
-                in_=src[:].rearrange("p t (c i) -> p c t i", i=4),
+                out=dst.rearrange("p (c i) t -> p c t i", i=4),
+                in_=src.rearrange("p t (c i) -> p c t i", i=4),
             )
 
         def regroup_z1(g):
-            dst = operands.tile([P, GROUP_F, PACK], BF16, name="z1_grouped", align_bytes=64)
-            regroup(nc.vector.tensor_copy if g < VECTOR_REGROUPS else nc.scalar.copy, dst, z1_sb[g])
+            dst = regrouped_z1.tile([P, GROUP_F, PACK], BF16, name="z1_grouped", align_bytes=64)
+            if g < VECTOR_REGROUPS:
+                regroup(nc.vector.tensor_copy, dst[:], z1_sb[g][:])
+            else:
+                for u in range(RUN):
+                    cols = slice(u * TILE_F, (u + 1) * TILE_F)
+                    nc.gpsimd.tensor_scalar(
+                        out=dst[:, cols, :],
+                        in0=z1_sb[g][:, :, cols].rearrange("p t f -> p f t"),
+                        scalar1=1.0,
+                        scalar2=0.0,
+                        op0=MULT,
+                        op1=ADD,
+                    )
             grouped[1, g] = dst
 
         def regroup_z2(g):
             dst = operands.tile([P, GROUP_F, PACK], BF16, name="z2_grouped", align_bytes=64)
-            regroup(nc.vector.tensor_copy, dst, z2_sb[g])
+            for u in range(RUN):
+                cols = slice(u * TILE_F, (u + 1) * TILE_F)
+                regroup(nc.vector.tensor_copy if u % 2 == 0 else nc.scalar.copy, dst[:, cols, :], z2_sb[g][:, :, cols])
             grouped[2, g] = dst
 
         def quantise(step, g):
@@ -157,14 +173,14 @@ def tile_manualchebconv_pb_kernel(tc, z0, z1, L_words, L_scales, out_0, out_1):
             if 0 <= g < GROUPS:
                 step_of_group(*args, g)
 
-        for r in range(-3, GROUPS + 1):
-            for_group(r - 1, multiply, 2)
-            for_group(r + 1, multiply, 1)
+        for r in range(-3, GROUPS + 2):
             for_group(r, first_combine)
             for_group(r, regroup_z2)
-            for_group(r - 1, turn, 2)
-            for_group(r - 1, second_combine)
-            for_group(r + 1, turn, 1)
-            for_group(r, quantise, 2)
             for_group(r + 2, quantise, 1)
+            for_group(r - 2, turn, 2)
+            for_group(r - 1, multiply, 2)
+            for_group(r - 2, second_combine)
+            for_group(r + 1, turn, 1)
+            for_group(r + 2, multiply, 1)
+            for_group(r, quantise, 2)
             for_group(r + 3, regroup_z1)

@@ -1,7 +1,6 @@
 from contextlib import ExitStack
 
 import concourse.mybir as mybir
-from concourse.masks import make_identity
 
 FP8X4 = mybir.dt.float8_e4m3fn_x4
 BF16 = mybir.dt.bfloat16
@@ -18,12 +17,13 @@ PACK = 4
 BATCH = 4
 NODES = P * PACK
 FEATURES = 1024
+GROUP_F = 512
 TILE_F = 128
-RUN = 4
-GROUP_F = RUN * TILE_F
 GROUPS_PER_ITEM = FEATURES // GROUP_F
 GROUPS = BATCH * GROUPS_PER_ITEM
-VECTOR_REGROUPS = 2
+SHARED_REGROUPS = 2
+HALVED_LOADS = {"z1": 2, "z0": 1}
+HELPED_BANK = 2
 
 FLOPS = 2 * 2 * BATCH * NODES * NODES * FEATURES
 
@@ -31,55 +31,88 @@ FLOPS = 2 * 2 * BATCH * NODES * NODES * FEATURES
 def tile_manualchebconv_pb_kernel(tc, z0, z1, L_words, L_scales, out_0, out_1):
     nc = tc.nc
 
-    def by_group(dram):
-        rows = dram.rearrange("b (p t) f -> b p t f", t=PACK)
-        return [
-            rows[g // GROUPS_PER_ITEM][:, :, (g % GROUPS_PER_ITEM) * GROUP_F : (g % GROUPS_PER_ITEM + 1) * GROUP_F]
-            for g in range(GROUPS)
-        ]
+    def by_item(dram):
+        return dram.rearrange("b (p t) f -> b p t f", t=PACK)
 
-    z0_dram, z1_dram = by_group(z0), by_group(z1)
-    z2_dram, z3_dram = by_group(out_0), by_group(out_1)
+    z0_dram, z1_dram, z2_dram, z3_dram = by_item(z0), by_item(z1), by_item(out_0), by_item(out_1)
+
+    def item_of(g):
+        return g // GROUPS_PER_ITEM
+
+    def cols_of(g):
+        h = g % GROUPS_PER_ITEM
+        return slice(h * GROUP_F, (h + 1) * GROUP_F)
 
     with ExitStack() as ctx:
         consts = ctx.enter_context(tc.tile_pool(name="consts", bufs=1))
         inputs = ctx.enter_context(tc.tile_pool(name="inputs", bufs=1))
-        regrouped_z1 = ctx.enter_context(tc.tile_pool(name="regrouped_z1", bufs=3))
-        operands = ctx.enter_context(tc.tile_pool(name="operands", bufs=2))
-        sorted_pool = ctx.enter_context(tc.tile_pool(name="sorted", bufs=3 * RUN))
-        results = ctx.enter_context(tc.tile_pool(name="results", bufs=4))
-        product_banks = ctx.enter_context(tc.psum_pool(name="product_banks", bufs=RUN))
-        turned_banks = ctx.enter_context(tc.psum_pool(name="turned_banks", bufs=RUN))
+        regrouped = ctx.enter_context(tc.tile_pool(name="regrouped", bufs=3))
+        operands = ctx.enter_context(tc.tile_pool(name="operands", bufs=3))
+        doubled_pool = ctx.enter_context(tc.tile_pool(name="doubled", bufs=3))
+        results = ctx.enter_context(tc.tile_pool(name="results", bufs=12))
+        banks = ctx.enter_context(tc.psum_pool(name="banks", bufs=8))
         ctx.enter_context(tc.manual_schedule())
 
-        identity = consts.tile([P, P], F32, name="identity")
-        make_identity(nc, identity[:])
-
+        l_words_raw = consts.tile([P, NODES], U32, name="l_words_raw", align_bytes=64)
+        l_scales_raw = consts.tile([P, NODES], U8, name="l_scales_raw", align_bytes=64)
+        nc.vector.memset(l_scales_raw[:].bitcast(I32), 0)
         l_words = consts.tile([P, NODES], U32, name="l_words", align_bytes=64)
         l_scales = consts.tile([P, NODES], U8, name="l_scales", align_bytes=64)
-        nc.vector.memset(l_scales[:].bitcast(I32), 0)
 
-        z0_sb = [inputs.tile([P, PACK, GROUP_F], BF16, name="z0_sb%d" % g) for g in range(GROUPS)]
-        z1_sb = [inputs.tile([P, PACK, GROUP_F], BF16, name="z1_sb%d" % g) for g in range(GROUPS)]
+        def load_plan(name, dram):
+            parts, loads = [], []
+            for i in range(BATCH):
+                if i < HALVED_LOADS[name]:
+                    for g in range(GROUPS_PER_ITEM * i, GROUPS_PER_ITEM * (i + 1)):
+                        half = inputs.tile([P, PACK, GROUP_F], BF16, name="%s_half%d" % (name, g))
+                        parts.append(half[:])
+                        loads.append((half[:], dram[i][:, :, cols_of(g)]))
+                else:
+                    whole = inputs.tile([P, PACK, FEATURES], BF16, name="%s_item%d" % (name, i))
+                    for g in range(GROUPS_PER_ITEM * i, GROUPS_PER_ITEM * (i + 1)):
+                        parts.append(whole[:, :, cols_of(g)])
+                    loads.append((whole[:], dram[i]))
+            return parts, loads
 
-        nc.sync.dma_start(out=z1_sb[0][:], in_=z1_dram[0])
-        nc.sync.dma_start(out=l_words[:].bitcast(I32), in_=L_words[0].rearrange("p n t -> p (n t)").bitcast(I32))
+        z0_sb, z0_loads = load_plan("z0", z0_dram)
+        z1_sb, z1_loads = load_plan("z1", z1_dram)
+
+        def load(pair):
+            nc.sync.dma_start(out=pair[0], in_=pair[1])
+
+        load(z1_loads[0])
+        nc.sync.dma_start(out=l_words_raw[:].bitcast(I32), in_=L_words[0].rearrange("p n t -> p (n t)").bitcast(I32))
         for quadrant in range(4):
             nc.sync.dma_start(
-                out=l_scales[32 * quadrant : 32 * quadrant + 4, :].bitcast(I32),
+                out=l_scales_raw[32 * quadrant : 32 * quadrant + 4, :].bitcast(I32),
                 in_=L_scales[0, 4 * quadrant : 4 * quadrant + 4, :].bitcast(I32),
             )
-        nc.sync.dma_start(out=z1_sb[1][:], in_=z1_dram[1])
-        for g in range(GROUPS):
-            nc.sync.dma_start(out=z0_sb[g][:], in_=z0_dram[g])
-            if g + 2 < GROUPS:
-                nc.sync.dma_start(out=z1_sb[g + 2][:], in_=z1_dram[g + 2])
+        load(z1_loads[1])
+        load(z0_loads[0])
+        load(z0_loads[1])
+        load(z1_loads[2])
+        load(z1_loads[3])
+        for k in range(2, len(z0_loads)):
+            load(z0_loads[k])
+            if k + 2 < len(z1_loads):
+                load(z1_loads[k + 2])
+
+        def sort_l_words():
+            nc.vector.tensor_copy(
+                out=l_words[:].bitcast(I32).rearrange("p (t m) -> p t m", t=PACK),
+                in_=l_words_raw[:].bitcast(I32).rearrange("p (m t) -> p t m", t=PACK),
+            )
+
+        def sort_l_scales():
+            nc.vector.tensor_copy(
+                out=l_scales[:].rearrange("p (t m) -> p t m", t=PACK),
+                in_=l_scales_raw[:].rearrange("p (m t) -> p t m", t=PACK),
+            )
 
         grouped = {}
         quantised = {}
-        sorted_products = {}
-        turned = {}
-        z2_sb = {}
+        products = {}
+        result_sb = {}
 
         def regroup(engine_copy, dst, src):
             engine_copy(
@@ -87,28 +120,27 @@ def tile_manualchebconv_pb_kernel(tc, z0, z1, L_words, L_scales, out_0, out_1):
                 in_=src.rearrange("p t (c i) -> p c t i", i=4),
             )
 
+        def regroup_on_gpsimd(dst, src):
+            nc.gpsimd.tensor_scalar(
+                out=dst, in0=src.rearrange("p t f -> p f t"), scalar1=1.0, scalar2=0.0, op0=MULT, op1=ADD
+            )
+
         def regroup_z1(g):
-            dst = regrouped_z1.tile([P, GROUP_F, PACK], BF16, name="z1_grouped", align_bytes=64)
-            if g < VECTOR_REGROUPS:
-                regroup(nc.vector.tensor_copy, dst[:], z1_sb[g][:])
-            else:
-                for u in range(RUN):
-                    cols = slice(u * TILE_F, (u + 1) * TILE_F)
-                    nc.gpsimd.tensor_scalar(
-                        out=dst[:, cols, :],
-                        in0=z1_sb[g][:, :, cols].rearrange("p t f -> p f t"),
-                        scalar1=1.0,
-                        scalar2=0.0,
-                        op0=MULT,
-                        op1=ADD,
-                    )
+            dst = regrouped.tile([P, GROUP_F, PACK], BF16, name="z1_grouped", align_bytes=64)
+            src = z1_sb[g]
+            for u in range(GROUP_F // TILE_F):
+                part = slice(u * TILE_F, (u + 1) * TILE_F)
+                if g < SHARED_REGROUPS and u < 2:
+                    regroup(nc.vector.tensor_copy, dst[:, part, :], src[:, :, part])
+                elif g < SHARED_REGROUPS and u == 2:
+                    regroup(nc.scalar.copy, dst[:, part, :], src[:, :, part])
+                else:
+                    regroup_on_gpsimd(dst[:, part, :], src[:, :, part])
             grouped[1, g] = dst
 
         def regroup_z2(g):
-            dst = operands.tile([P, GROUP_F, PACK], BF16, name="z2_grouped", align_bytes=64)
-            for u in range(RUN):
-                cols = slice(u * TILE_F, (u + 1) * TILE_F)
-                regroup(nc.vector.tensor_copy if u % 2 == 0 else nc.scalar.copy, dst[:, cols, :], z2_sb[g][:, :, cols])
+            dst = regrouped.tile([P, GROUP_F, PACK], BF16, name="z2_grouped", align_bytes=64)
+            regroup(nc.scalar.copy, dst[:], result_sb[1, g][:])
             grouped[2, g] = dst
 
         def quantise(step, g):
@@ -123,48 +155,46 @@ def tile_manualchebconv_pb_kernel(tc, z0, z1, L_words, L_scales, out_0, out_1):
 
         def multiply(step, g):
             codes, scales = quantised[step, g]
-            sorted_products[step, g] = []
-            for u in range(RUN):
-                cols = slice(u * TILE_F, (u + 1) * TILE_F)
-                product = product_banks.tile([P, NODES], F32, name="product")
+            products[step, g] = []
+            for t in range(PACK):
+                sorted_cols = slice(t * P, (t + 1) * P)
+                bank = banks.tile([P, GROUP_F], F32, name="bank")
                 nc.tensor.matmul_mx(
-                    out=product[:],
-                    lhsT=codes[:, cols].bitcast(FP8X4),
-                    lhsT_scale=scales[:, cols],
-                    rhs=l_words[:].bitcast(FP8X4),
-                    rhs_scale=l_scales[:],
+                    out=bank[:],
+                    lhsT=l_words[:, sorted_cols].bitcast(FP8X4),
+                    lhsT_scale=l_scales[:, sorted_cols],
+                    rhs=codes[:].bitcast(FP8X4),
+                    rhs_scale=scales[:],
                     start=True,
                     stop=True,
                 )
-                by_t = sorted_pool.tile([P, PACK, P], F32, name="by_t")
-                nc.scalar.copy(out=by_t[:], in_=product[:].rearrange("f (p t) -> f t p", t=PACK))
-                sorted_products[step, g].append(by_t)
-
-        def turn(step, g):
-            turned[step, g] = []
-            for u in range(RUN):
-                bank = turned_banks.tile([P, PACK, TILE_F], F32, name="bank")
-                for t in range(PACK):
-                    nc.tensor.transpose(bank[:, t, :], sorted_products[step, g][u][:, t, :], identity[:])
-                turned[step, g].append(bank)
+                products[step, g].append(bank)
 
         def combine(step, g, older, dram):
-            result = results.tile([P, PACK, GROUP_F], F32, name="result%d" % step)
-            for u in range(RUN):
-                cols = slice(u * TILE_F, (u + 1) * TILE_F)
-                nc.vector.scalar_tensor_tensor(
-                    out=result[:, :, cols],
-                    in0=turned[step, g][u][:],
-                    scalar=2.0,
-                    in1=older[g][:, :, cols],
-                    op0=MULT,
-                    op1=SUBTRACT,
-                )
-            nc.sync.dma_start(out=dram[g], in_=result[:])
-            return result
+            result = results.tile([P, PACK, GROUP_F], F32, name="result")
+            result_sb[step, g] = result
+            last = step == 2 and g == GROUPS - 1
+            for t in range(PACK):
+                if step == 2 and t == HELPED_BANK and not last:
+                    doubled = doubled_pool.tile([P, GROUP_F], F32, name="doubled")
+                    nc.scalar.mul(doubled[:], products[step, g][t][:], 2.0)
+                    nc.gpsimd.tensor_tensor(out=result[:, t, :], in0=doubled[:], in1=older[g][:, t, :], op=SUBTRACT)
+                else:
+                    nc.vector.scalar_tensor_tensor(
+                        out=result[:, t, :],
+                        in0=products[step, g][t][:],
+                        scalar=2.0,
+                        in1=older[g][:, t, :],
+                        op0=MULT,
+                        op1=SUBTRACT,
+                    )
+                if last:
+                    nc.sync.dma_start(out=dram[item_of(g)][:, t, cols_of(g)], in_=result[:, t, :])
+            if not last:
+                nc.sync.dma_start(out=dram[item_of(g)][:, :, cols_of(g)], in_=result[:])
 
         def first_combine(g):
-            z2_sb[g] = combine(1, g, z0_sb, z2_dram)
+            combine(1, g, z0_sb, z2_dram)
 
         def second_combine(g):
             combine(2, g, z1_sb, z3_dram)
@@ -173,14 +203,21 @@ def tile_manualchebconv_pb_kernel(tc, z0, z1, L_words, L_scales, out_0, out_1):
             if 0 <= g < GROUPS:
                 step_of_group(*args, g)
 
-        for r in range(-3, GROUPS + 2):
+        regroup_z1(0)
+        sort_l_words()
+        quantise(1, 0)
+        sort_l_scales()
+        multiply(1, 0)
+        regroup_z1(1)
+        quantise(1, 1)
+        multiply(1, 1)
+        for r in range(GROUPS + 1):
             for_group(r, first_combine)
             for_group(r, regroup_z2)
-            for_group(r + 2, quantise, 1)
-            for_group(r - 2, turn, 2)
+            for_group(r - 1, quantise, 2)
             for_group(r - 1, multiply, 2)
-            for_group(r - 2, second_combine)
-            for_group(r + 1, turn, 1)
-            for_group(r + 2, multiply, 1)
-            for_group(r, quantise, 2)
-            for_group(r + 3, regroup_z1)
+            if r >= 1:
+                for_group(r + 1, quantise, 1)
+                for_group(r + 1, multiply, 1)
+            for_group(r + 2, regroup_z1)
+            for_group(r - 1, second_combine)

@@ -115,10 +115,7 @@ def tile_manualchebconv_pb_kernel(tc, z0, z1, L_words, L_scales, out_0, out_1):
         result_sb = {}
 
         def regroup(engine_copy, dst, src):
-            engine_copy(
-                out=dst.rearrange("p (c i) t -> p c t i", i=4),
-                in_=src.rearrange("p t (c i) -> p c t i", i=4),
-            )
+            engine_copy(out=dst, in_=src.rearrange("p t f -> p f t"))
 
         def regroup_on_gpsimd(dst, src):
             nc.gpsimd.tensor_scalar(

@@ -9,7 +9,6 @@ I32 = mybir.dt.int32
 U32 = mybir.dt.uint32
 U8 = mybir.dt.uint8
 MULT = mybir.AluOpType.mult
-ADD = mybir.AluOpType.add
 SUBTRACT = mybir.AluOpType.subtract
 
 P = 128
@@ -18,12 +17,10 @@ BATCH = 4
 NODES = P * PACK
 FEATURES = 1024
 GROUP_F = 512
-TILE_F = 128
 GROUPS_PER_ITEM = FEATURES // GROUP_F
 GROUPS = BATCH * GROUPS_PER_ITEM
 SHARED_REGROUPS = 2
 HALVED_LOADS = {"z1": 2, "z0": 1}
-HELPED_BANK = 2
 
 FLOPS = 2 * 2 * BATCH * NODES * NODES * FEATURES
 
@@ -48,7 +45,6 @@ def tile_manualchebconv_pb_kernel(tc, z0, z1, L_words, L_scales, out_0, out_1):
         inputs = ctx.enter_context(tc.tile_pool(name="inputs", bufs=1))
         regrouped = ctx.enter_context(tc.tile_pool(name="regrouped", bufs=3))
         operands = ctx.enter_context(tc.tile_pool(name="operands", bufs=3))
-        doubled_pool = ctx.enter_context(tc.tile_pool(name="doubled", bufs=3))
         results = ctx.enter_context(tc.tile_pool(name="results", bufs=12))
         banks = ctx.enter_context(tc.psum_pool(name="banks", bufs=8))
         ctx.enter_context(tc.manual_schedule())
@@ -117,22 +113,15 @@ def tile_manualchebconv_pb_kernel(tc, z0, z1, L_words, L_scales, out_0, out_1):
         def regroup(engine_copy, dst, src):
             engine_copy(out=dst, in_=src.rearrange("p t f -> p f t"))
 
-        def regroup_on_gpsimd(dst, src):
-            nc.gpsimd.tensor_scalar(
-                out=dst, in0=src.rearrange("p t f -> p f t"), scalar1=1.0, scalar2=0.0, op0=MULT, op1=ADD
-            )
-
         def regroup_z1(g):
             dst = regrouped.tile([P, GROUP_F, PACK], BF16, name="z1_grouped", align_bytes=64)
             src = z1_sb[g]
-            for u in range(GROUP_F // TILE_F):
-                part = slice(u * TILE_F, (u + 1) * TILE_F)
-                if g < SHARED_REGROUPS and u < 2:
-                    regroup(nc.vector.tensor_copy, dst[:, part, :], src[:, :, part])
-                elif g < SHARED_REGROUPS and u == 2:
-                    regroup(nc.scalar.copy, dst[:, part, :], src[:, :, part])
-                else:
-                    regroup_on_gpsimd(dst[:, part, :], src[:, :, part])
+            if g < SHARED_REGROUPS:
+                cut = 3 * GROUP_F // 4
+                regroup(nc.vector.tensor_copy, dst[:, :cut, :], src[:, :, :cut])
+                regroup(nc.scalar.copy, dst[:, cut:, :], src[:, :, cut:])
+            else:
+                regroup(nc.scalar.copy, dst[:], src)
             grouped[1, g] = dst
 
         def regroup_z2(g):
@@ -172,19 +161,14 @@ def tile_manualchebconv_pb_kernel(tc, z0, z1, L_words, L_scales, out_0, out_1):
             result_sb[step, g] = result
             last = step == 2 and g == GROUPS - 1
             for t in range(PACK):
-                if step == 2 and t == HELPED_BANK and not last:
-                    doubled = doubled_pool.tile([P, GROUP_F], F32, name="doubled")
-                    nc.scalar.mul(doubled[:], products[step, g][t][:], 2.0)
-                    nc.gpsimd.tensor_tensor(out=result[:, t, :], in0=doubled[:], in1=older[g][:, t, :], op=SUBTRACT)
-                else:
-                    nc.vector.scalar_tensor_tensor(
-                        out=result[:, t, :],
-                        in0=products[step, g][t][:],
-                        scalar=2.0,
-                        in1=older[g][:, t, :],
-                        op0=MULT,
-                        op1=SUBTRACT,
-                    )
+                nc.vector.scalar_tensor_tensor(
+                    out=result[:, t, :],
+                    in0=products[step, g][t][:],
+                    scalar=2.0,
+                    in1=older[g][:, t, :],
+                    op0=MULT,
+                    op1=SUBTRACT,
+                )
                 if last:
                     nc.sync.dma_start(out=dram[item_of(g)][:, t, cols_of(g)], in_=result[:, t, :])
             if not last:

@@ -9,6 +9,7 @@ I32 = mybir.dt.int32
 U32 = mybir.dt.uint32
 U8 = mybir.dt.uint8
 MULT = mybir.AluOpType.mult
+ADD = mybir.AluOpType.add
 SUBTRACT = mybir.AluOpType.subtract
 
 P = 128
@@ -20,6 +21,8 @@ GROUP_F = 512
 GROUPS_PER_ITEM = FEATURES // GROUP_F
 GROUPS = BATCH * GROUPS_PER_ITEM
 SHARED_REGROUPS = 2
+GPSIMD_F = 128
+HELPED_BANK = 2
 HALVED_LOADS = {"z1": 2, "z0": 1}
 
 FLOPS = 2 * 2 * BATCH * NODES * NODES * FEATURES
@@ -43,7 +46,9 @@ def tile_manualchebconv_pb_kernel(tc, z0, z1, L_words, L_scales, out_0, out_1):
     with ExitStack() as ctx:
         consts = ctx.enter_context(tc.tile_pool(name="consts", bufs=1))
         inputs = ctx.enter_context(tc.tile_pool(name="inputs", bufs=1))
+        regrouped_z1 = ctx.enter_context(tc.tile_pool(name="regrouped_z1", bufs=1))
         regrouped = ctx.enter_context(tc.tile_pool(name="regrouped", bufs=3))
+        doubled_pool = ctx.enter_context(tc.tile_pool(name="doubled", bufs=2))
         operands = ctx.enter_context(tc.tile_pool(name="operands", bufs=3))
         results = ctx.enter_context(tc.tile_pool(name="results", bufs=12))
         banks = ctx.enter_context(tc.psum_pool(name="banks", bufs=8))
@@ -113,16 +118,28 @@ def tile_manualchebconv_pb_kernel(tc, z0, z1, L_words, L_scales, out_0, out_1):
         def regroup(engine_copy, dst, src):
             engine_copy(out=dst, in_=src.rearrange("p t f -> p f t"))
 
-        def regroup_z1(g):
-            dst = regrouped.tile([P, GROUP_F, PACK], BF16, name="z1_grouped", align_bytes=64)
+        def regroup_z1_first_part(g):
+            dst = regrouped_z1.tile([P, GROUP_F, PACK], BF16, name="z1_grouped", align_bytes=64)
+            grouped[1, g] = dst
             src = z1_sb[g]
             if g < SHARED_REGROUPS:
                 cut = 3 * GROUP_F // 4
                 regroup(nc.vector.tensor_copy, dst[:, :cut, :], src[:, :, :cut])
                 regroup(nc.scalar.copy, dst[:, cut:, :], src[:, :, cut:])
             else:
-                regroup(nc.scalar.copy, dst[:], src)
-            grouped[1, g] = dst
+                for f0 in range(GROUP_F // 2, GROUP_F, GPSIMD_F):
+                    nc.gpsimd.tensor_scalar(
+                        out=dst[:, f0 : f0 + GPSIMD_F, :],
+                        in0=src[:, :, f0 : f0 + GPSIMD_F].rearrange("p t f -> p f t"),
+                        scalar1=1.0,
+                        scalar2=0.0,
+                        op0=MULT,
+                        op1=ADD,
+                    )
+
+        def regroup_z1_second_part(g):
+            if g >= SHARED_REGROUPS:
+                regroup(nc.scalar.copy, grouped[1, g][:, : GROUP_F // 2, :], z1_sb[g][:, :, : GROUP_F // 2])
 
         def regroup_z2(g):
             dst = regrouped.tile([P, GROUP_F, PACK], BF16, name="z2_grouped", align_bytes=64)
@@ -161,14 +178,22 @@ def tile_manualchebconv_pb_kernel(tc, z0, z1, L_words, L_scales, out_0, out_1):
             result_sb[step, g] = result
             last = step == 2 and g == GROUPS - 1
             for t in range(PACK):
-                nc.vector.scalar_tensor_tensor(
-                    out=result[:, t, :],
-                    in0=products[step, g][t][:],
-                    scalar=2.0,
-                    in1=older[g][:, t, :],
-                    op0=MULT,
-                    op1=SUBTRACT,
-                )
+                if step == 2 and t == HELPED_BANK and not last:
+                    doubled = doubled_pool.tile([P, GROUP_F], F32, name="doubled")
+                    nc.scalar.mul(doubled[:], products[step, g][t][:], 2.0)
+                    for part in (slice(0, GROUP_F // 2), slice(GROUP_F // 2, GROUP_F)):
+                        nc.gpsimd.tensor_tensor(
+                            out=result[:, t, part], in0=doubled[:, part], in1=older[g][:, t, part], op=SUBTRACT
+                        )
+                else:
+                    nc.vector.scalar_tensor_tensor(
+                        out=result[:, t, :],
+                        in0=products[step, g][t][:],
+                        scalar=2.0,
+                        in1=older[g][:, t, :],
+                        op0=MULT,
+                        op1=SUBTRACT,
+                    )
                 if last:
                     nc.sync.dma_start(out=dram[item_of(g)][:, t, cols_of(g)], in_=result[:, t, :])
             if not last:
@@ -184,12 +209,12 @@ def tile_manualchebconv_pb_kernel(tc, z0, z1, L_words, L_scales, out_0, out_1):
             if 0 <= g < GROUPS:
                 step_of_group(*args, g)
 
-        regroup_z1(0)
+        regroup_z1_first_part(0)
         sort_l_words()
         quantise(1, 0)
         sort_l_scales()
         multiply(1, 0)
-        regroup_z1(1)
+        regroup_z1_first_part(1)
         quantise(1, 1)
         multiply(1, 1)
         for r in range(GROUPS + 1):
@@ -200,5 +225,6 @@ def tile_manualchebconv_pb_kernel(tc, z0, z1, L_words, L_scales, out_0, out_1):
             if r >= 1:
                 for_group(r + 1, quantise, 1)
                 for_group(r + 1, multiply, 1)
-            for_group(r + 2, regroup_z1)
+            for_group(r + 2, regroup_z1_first_part)
             for_group(r - 1, second_combine)
+            for_group(r + 2, regroup_z1_second_part)

@@ -22,7 +22,8 @@ GROUPS_PER_ITEM = FEATURES // GROUP_F
 GROUPS = BATCH * GROUPS_PER_ITEM
 SHARED_REGROUPS = 2
 GPSIMD_F = 128
-HELPED_BANK = 2
+HELPED_BANK = 3
+LAG = 3
 HALVED_LOADS = {"z1": 2, "z0": 1}
 
 FLOPS = 2 * 2 * BATCH * NODES * NODES * FEATURES
@@ -90,8 +91,8 @@ def tile_manualchebconv_pb_kernel(tc, z0, z1, L_words, L_scales, out_0, out_1):
             )
         load(z1_loads[1])
         load(z0_loads[0])
-        load(z0_loads[1])
         load(z1_loads[2])
+        load(z0_loads[1])
         load(z1_loads[3])
         for k in range(2, len(z0_loads)):
             load(z0_loads[k])
@@ -118,7 +119,7 @@ def tile_manualchebconv_pb_kernel(tc, z0, z1, L_words, L_scales, out_0, out_1):
         def regroup(engine_copy, dst, src):
             engine_copy(out=dst, in_=src.rearrange("p t f -> p f t"))
 
-        def regroup_z1_first_part(g):
+        def regroup_z1(g):
             dst = regrouped_z1.tile([P, GROUP_F, PACK], BF16, name="z1_grouped", align_bytes=64)
             grouped[1, g] = dst
             src = z1_sb[g]
@@ -136,10 +137,7 @@ def tile_manualchebconv_pb_kernel(tc, z0, z1, L_words, L_scales, out_0, out_1):
                         op0=MULT,
                         op1=ADD,
                     )
-
-        def regroup_z1_second_part(g):
-            if g >= SHARED_REGROUPS:
-                regroup(nc.scalar.copy, grouped[1, g][:, : GROUP_F // 2, :], z1_sb[g][:, :, : GROUP_F // 2])
+                regroup(nc.scalar.copy, dst[:, : GROUP_F // 2, :], src[:, :, : GROUP_F // 2])
 
         def regroup_z2(g):
             dst = regrouped.tile([P, GROUP_F, PACK], BF16, name="z2_grouped", align_bytes=64)
@@ -177,8 +175,8 @@ def tile_manualchebconv_pb_kernel(tc, z0, z1, L_words, L_scales, out_0, out_1):
             result = results.tile([P, PACK, GROUP_F], F32, name="result")
             result_sb[step, g] = result
             last = step == 2 and g == GROUPS - 1
-            for t in range(PACK):
-                if step == 2 and t == HELPED_BANK and not last:
+            for t in (HELPED_BANK, 0, 1, 2) if step == 2 else range(PACK):
+                if step == 2 and t == HELPED_BANK:
                     doubled = doubled_pool.tile([P, GROUP_F], F32, name="doubled")
                     nc.scalar.mul(doubled[:], products[step, g][t][:], 2.0)
                     for part in (slice(0, GROUP_F // 2), slice(GROUP_F // 2, GROUP_F)):
@@ -194,37 +192,41 @@ def tile_manualchebconv_pb_kernel(tc, z0, z1, L_words, L_scales, out_0, out_1):
                         op0=MULT,
                         op1=SUBTRACT,
                     )
-                if last:
+                if last and t != HELPED_BANK:
                     nc.sync.dma_start(out=dram[item_of(g)][:, t, cols_of(g)], in_=result[:, t, :])
+            if last:
+                nc.sync.dma_start(out=dram[item_of(g)][:, HELPED_BANK, cols_of(g)], in_=result[:, HELPED_BANK, :])
             if not last:
                 nc.sync.dma_start(out=dram[item_of(g)][:, :, cols_of(g)], in_=result[:])
 
-        def first_combine(g):
-            combine(1, g, z0_sb, z2_dram)
+        older_of = {1: z0_sb, 2: z1_sb}
+        dram_of = {1: z2_dram, 2: z3_dram}
 
-        def second_combine(g):
-            combine(2, g, z1_sb, z3_dram)
+        order = []
+        for g in range(GROUPS + LAG):
+            if g < GROUPS:
+                order.append((1, g))
+            if g >= LAG:
+                order.append((2, g - LAG))
 
-        def for_group(g, step_of_group, *args):
-            if 0 <= g < GROUPS:
-                step_of_group(*args, g)
-
-        regroup_z1_first_part(0)
+        regroup_z1(0)
         sort_l_words()
         quantise(1, 0)
         sort_l_scales()
         multiply(1, 0)
-        regroup_z1_first_part(1)
-        quantise(1, 1)
-        multiply(1, 1)
-        for r in range(GROUPS + 1):
-            for_group(r, first_combine)
-            for_group(r, regroup_z2)
-            for_group(r - 1, quantise, 2)
-            for_group(r - 1, multiply, 2)
-            if r >= 1:
-                for_group(r + 1, quantise, 1)
-                for_group(r + 1, multiply, 1)
-            for_group(r + 2, regroup_z1_first_part)
-            for_group(r - 1, second_combine)
-            for_group(r + 2, regroup_z1_second_part)
+        regroup_z1(1)
+        combined = []
+        for j in range(len(order)):
+            step, g = order[j]
+            if j + 1 < len(order):
+                next_step, next_g = order[j + 1]
+                quantise(next_step, next_g)
+                multiply(next_step, next_g)
+                if next_step == 1 and next_g + 1 < GROUPS:
+                    regroup_z1(next_g + 1)
+            for waiting in combined:
+                regroup_z2(waiting)
+            combined.clear()
+            combine(step, g, older_of[step], dram_of[step])
+            if step == 1:
+                combined.append(g)

@@ -22,7 +22,6 @@ GROUPS_PER_ITEM = FEATURES // GROUP_F
 GROUPS = BATCH * GROUPS_PER_ITEM
 SHARED_REGROUPS = 2
 GPSIMD_F = 128
-HELPED_BANK = 3
 LAG = 3
 HALVED_LOADS = {"z1": 2, "z0": 1}
 
@@ -49,7 +48,6 @@ def tile_manualchebconv_pb_kernel(tc, z0, z1, L_words, L_scales, out_0, out_1):
         inputs = ctx.enter_context(tc.tile_pool(name="inputs", bufs=1))
         regrouped_z1 = ctx.enter_context(tc.tile_pool(name="regrouped_z1", bufs=1))
         regrouped = ctx.enter_context(tc.tile_pool(name="regrouped", bufs=3))
-        doubled_pool = ctx.enter_context(tc.tile_pool(name="doubled", bufs=2))
         operands = ctx.enter_context(tc.tile_pool(name="operands", bufs=3))
         results = ctx.enter_context(tc.tile_pool(name="results", bufs=12))
         banks = ctx.enter_context(tc.psum_pool(name="banks", bufs=8))
@@ -175,27 +173,17 @@ def tile_manualchebconv_pb_kernel(tc, z0, z1, L_words, L_scales, out_0, out_1):
             result = results.tile([P, PACK, GROUP_F], F32, name="result")
             result_sb[step, g] = result
             last = step == 2 and g == GROUPS - 1
-            for t in (HELPED_BANK, 0, 1, 2) if step == 2 else range(PACK):
-                if step == 2 and t == HELPED_BANK:
-                    doubled = doubled_pool.tile([P, GROUP_F], F32, name="doubled")
-                    nc.scalar.mul(doubled[:], products[step, g][t][:], 2.0)
-                    for part in (slice(0, GROUP_F // 2), slice(GROUP_F // 2, GROUP_F)):
-                        nc.gpsimd.tensor_tensor(
-                            out=result[:, t, part], in0=doubled[:, part], in1=older[g][:, t, part], op=SUBTRACT
-                        )
-                else:
-                    nc.vector.scalar_tensor_tensor(
-                        out=result[:, t, :],
-                        in0=products[step, g][t][:],
-                        scalar=2.0,
-                        in1=older[g][:, t, :],
-                        op0=MULT,
-                        op1=SUBTRACT,
-                    )
-                if last and t != HELPED_BANK:
+            for t in range(PACK):
+                nc.vector.scalar_tensor_tensor(
+                    out=result[:, t, :],
+                    in0=products[step, g][t][:],
+                    scalar=2.0,
+                    in1=older[g][:, t, :],
+                    op0=MULT,
+                    op1=SUBTRACT,
+                )
+                if last:
                     nc.sync.dma_start(out=dram[item_of(g)][:, t, cols_of(g)], in_=result[:, t, :])
-            if last:
-                nc.sync.dma_start(out=dram[item_of(g)][:, HELPED_BANK, cols_of(g)], in_=result[:, HELPED_BANK, :])
             if not last:
                 nc.sync.dma_start(out=dram[item_of(g)][:, :, cols_of(g)], in_=result[:])
 

@@ -17,13 +17,9 @@ PACK = 4
 BATCH = 4
 NODES = P * PACK
 FEATURES = 1024
-GROUP_F = 512
-GROUPS_PER_ITEM = FEATURES // GROUP_F
-GROUPS = BATCH * GROUPS_PER_ITEM
-SHARED_REGROUPS = 2
+HALF_F = 512
+HALVES = FEATURES // HALF_F
 GPSIMD_F = 128
-LAG = 3
-HALVED_LOADS = {"z1": 2, "z0": 1}
 
 FLOPS = 2 * 2 * BATCH * NODES * NODES * FEATURES
 
@@ -36,20 +32,16 @@ def tile_manualchebconv_pb_kernel(tc, z0, z1, L_words, L_scales, out_0, out_1):
 
     z0_dram, z1_dram, z2_dram, z3_dram = by_item(z0), by_item(z1), by_item(out_0), by_item(out_1)
 
-    def item_of(g):
-        return g // GROUPS_PER_ITEM
-
-    def cols_of(g):
-        h = g % GROUPS_PER_ITEM
-        return slice(h * GROUP_F, (h + 1) * GROUP_F)
+    def cols_of(h):
+        return slice(h * HALF_F, (h + 1) * HALF_F)
 
     with ExitStack() as ctx:
         consts = ctx.enter_context(tc.tile_pool(name="consts", bufs=1))
         inputs = ctx.enter_context(tc.tile_pool(name="inputs", bufs=1))
         regrouped_z1 = ctx.enter_context(tc.tile_pool(name="regrouped_z1", bufs=1))
-        regrouped = ctx.enter_context(tc.tile_pool(name="regrouped", bufs=3))
-        operands = ctx.enter_context(tc.tile_pool(name="operands", bufs=3))
-        results = ctx.enter_context(tc.tile_pool(name="results", bufs=12))
+        regrouped_z2 = ctx.enter_context(tc.tile_pool(name="regrouped_z2", bufs=4))
+        operands = ctx.enter_context(tc.tile_pool(name="operands", bufs=4))
+        results = ctx.enter_context(tc.tile_pool(name="results", bufs=7))
         banks = ctx.enter_context(tc.psum_pool(name="banks", bufs=8))
         ctx.enter_context(tc.manual_schedule())
 
@@ -59,43 +51,25 @@ def tile_manualchebconv_pb_kernel(tc, z0, z1, L_words, L_scales, out_0, out_1):
         l_words = consts.tile([P, NODES], U32, name="l_words", align_bytes=64)
         l_scales = consts.tile([P, NODES], U8, name="l_scales", align_bytes=64)
 
-        def load_plan(name, dram):
-            parts, loads = [], []
-            for i in range(BATCH):
-                if i < HALVED_LOADS[name]:
-                    for g in range(GROUPS_PER_ITEM * i, GROUPS_PER_ITEM * (i + 1)):
-                        half = inputs.tile([P, PACK, GROUP_F], BF16, name="%s_half%d" % (name, g))
-                        parts.append(half[:])
-                        loads.append((half[:], dram[i][:, :, cols_of(g)]))
-                else:
-                    whole = inputs.tile([P, PACK, FEATURES], BF16, name="%s_item%d" % (name, i))
-                    for g in range(GROUPS_PER_ITEM * i, GROUPS_PER_ITEM * (i + 1)):
-                        parts.append(whole[:, :, cols_of(g)])
-                    loads.append((whole[:], dram[i]))
-            return parts, loads
+        z0_sb, z1_sb = [], []
+        for i in range(BATCH):
+            z0_item = inputs.tile([P, PACK, FEATURES], BF16, name="z0_item%d" % i)
+            z1_item = inputs.tile([P, PACK, FEATURES], BF16, name="z1_item%d" % i)
+            z0_sb.append(z0_item)
+            z1_sb.append(z1_item)
 
-        z0_sb, z0_loads = load_plan("z0", z0_dram)
-        z1_sb, z1_loads = load_plan("z1", z1_dram)
-
-        def load(pair):
-            nc.sync.dma_start(out=pair[0], in_=pair[1])
-
-        load(z1_loads[0])
+        nc.sync.dma_start(out=z1_sb[0][:], in_=z1_dram[0])
         nc.sync.dma_start(out=l_words_raw[:].bitcast(I32), in_=L_words[0].rearrange("p n t -> p (n t)").bitcast(I32))
         for quadrant in range(4):
             nc.sync.dma_start(
                 out=l_scales_raw[32 * quadrant : 32 * quadrant + 4, :].bitcast(I32),
                 in_=L_scales[0, 4 * quadrant : 4 * quadrant + 4, :].bitcast(I32),
             )
-        load(z1_loads[1])
-        load(z0_loads[0])
-        load(z1_loads[2])
-        load(z0_loads[1])
-        load(z1_loads[3])
-        for k in range(2, len(z0_loads)):
-            load(z0_loads[k])
-            if k + 2 < len(z1_loads):
-                load(z1_loads[k + 2])
+        for rows in (slice(0, 2), slice(2, 4)):
+            nc.sync.dma_start(out=z0_sb[0][:, rows, :], in_=z0_dram[0][:, rows, :])
+        for i in range(1, BATCH):
+            nc.sync.dma_start(out=z1_sb[i][:], in_=z1_dram[i])
+            nc.sync.dma_start(out=z0_sb[i][:], in_=z0_dram[i])
 
         def sort_l_words():
             nc.vector.tensor_copy(
@@ -113,20 +87,24 @@ def tile_manualchebconv_pb_kernel(tc, z0, z1, L_words, L_scales, out_0, out_1):
         quantised = {}
         products = {}
         result_sb = {}
+        older_of = {1: z0_sb, 2: z1_sb}
+        dram_of = {1: z2_dram, 2: z3_dram}
 
         def regroup(engine_copy, dst, src):
             engine_copy(out=dst, in_=src.rearrange("p t f -> p f t"))
 
-        def regroup_z1(g):
-            dst = regrouped_z1.tile([P, GROUP_F, PACK], BF16, name="z1_grouped", align_bytes=64)
-            grouped[1, g] = dst
-            src = z1_sb[g]
-            if g < SHARED_REGROUPS:
-                cut = 3 * GROUP_F // 4
-                regroup(nc.vector.tensor_copy, dst[:, :cut, :], src[:, :, :cut])
-                regroup(nc.scalar.copy, dst[:, cut:, :], src[:, :, cut:])
-            else:
-                for f0 in range(GROUP_F // 2, GROUP_F, GPSIMD_F):
+        def regroup_z1(i):
+            item = regrouped_z1.tile([P, HALVES, HALF_F, PACK], BF16, name="z1_grouped", align_bytes=64)
+            for h in range(HALVES):
+                dst = item[:, h, :, :]
+                src = z1_sb[i][:, :, cols_of(h)]
+                grouped[1, i, h] = dst
+                if i == 0 and h == 0:
+                    cut = 5 * HALF_F // 8
+                    regroup(nc.vector.tensor_copy, dst[:, :cut, :], src[:, :, :cut])
+                    regroup(nc.scalar.copy, dst[:, cut:, :], src[:, :, cut:])
+                    continue
+                for f0 in range(HALF_F // 2, HALF_F, GPSIMD_F):
                     nc.gpsimd.tensor_scalar(
                         out=dst[:, f0 : f0 + GPSIMD_F, :],
                         in0=src[:, :, f0 : f0 + GPSIMD_F].rearrange("p t f -> p f t"),
@@ -135,86 +113,112 @@ def tile_manualchebconv_pb_kernel(tc, z0, z1, L_words, L_scales, out_0, out_1):
                         op0=MULT,
                         op1=ADD,
                     )
-                regroup(nc.scalar.copy, dst[:, : GROUP_F // 2, :], src[:, :, : GROUP_F // 2])
+                regroup(nc.scalar.copy, dst[:, : HALF_F // 2, :], src[:, :, : HALF_F // 2])
 
-        def regroup_z2(g):
-            dst = regrouped.tile([P, GROUP_F, PACK], BF16, name="z2_grouped", align_bytes=64)
-            regroup(nc.scalar.copy, dst[:], result_sb[1, g][:])
-            grouped[2, g] = dst
+        def regroup_z2(i):
+            for h in range(HALVES):
+                half = regrouped_z2.tile([P, HALF_F, PACK], BF16, name="z2_grouped", align_bytes=64)
+                regroup(nc.scalar.copy, half[:], result_sb[1, i][:, :, cols_of(h)])
+                grouped[2, i, h] = half[:]
 
-        def quantise(step, g):
-            codes = operands.tile([P, GROUP_F], U32, name="codes%d" % step, align_bytes=64)
-            scales = operands.tile([P, GROUP_F], U8, name="scales%d" % step, align_bytes=64)
+        def quantise(step, i, h):
+            codes = operands.tile([P, HALF_F], U32, name="codes%d" % step, align_bytes=64)
+            scales = operands.tile([P, HALF_F], U8, name="scales%d" % step, align_bytes=64)
             nc.vector.quantize_mx(
                 out=codes[:].bitcast(FP8X4),
                 scales=scales[:],
-                in_=grouped[step, g][:].rearrange("p f t -> p (f t)"),
+                in_=grouped[step, i, h].rearrange("p f t -> p (f t)"),
             )
-            quantised[step, g] = (codes, scales)
+            quantised[step, i, h] = (codes, scales)
 
-        def multiply(step, g):
-            codes, scales = quantised[step, g]
-            products[step, g] = []
-            for t in range(PACK):
-                sorted_cols = slice(t * P, (t + 1) * P)
-                bank = banks.tile([P, GROUP_F], F32, name="bank")
-                nc.tensor.matmul_mx(
-                    out=bank[:],
-                    lhsT=l_words[:, sorted_cols].bitcast(FP8X4),
-                    lhsT_scale=l_scales[:, sorted_cols],
-                    rhs=codes[:].bitcast(FP8X4),
-                    rhs_scale=scales[:],
-                    start=True,
-                    stop=True,
-                )
-                products[step, g].append(bank)
+        def multiply(step, i, t, h):
+            codes, scales = quantised[step, i, h]
+            sorted_cols = slice(t * P, (t + 1) * P)
+            bank = banks.tile([P, HALF_F], F32, name="bank")
+            nc.tensor.matmul_mx(
+                out=bank[:],
+                lhsT=l_words[:, sorted_cols].bitcast(FP8X4),
+                lhsT_scale=l_scales[:, sorted_cols],
+                rhs=codes[:].bitcast(FP8X4),
+                rhs_scale=scales[:],
+                start=True,
+                stop=True,
+            )
+            products[step, i, t, h] = bank
 
-        def combine(step, g, older, dram):
-            result = results.tile([P, PACK, GROUP_F], F32, name="result")
-            result_sb[step, g] = result
-            last = step == 2 and g == GROUPS - 1
-            for t in range(PACK):
-                nc.vector.scalar_tensor_tensor(
-                    out=result[:, t, :],
-                    in0=products[step, g][t][:],
-                    scalar=2.0,
-                    in1=older[g][:, t, :],
-                    op0=MULT,
-                    op1=SUBTRACT,
-                )
-                if last:
-                    nc.sync.dma_start(out=dram[item_of(g)][:, t, cols_of(g)], in_=result[:, t, :])
-            if not last:
-                nc.sync.dma_start(out=dram[item_of(g)][:, :, cols_of(g)], in_=result[:])
+        def combine(step, i, t, h):
+            if (step, i) not in result_sb:
+                result = results.tile([P, PACK, FEATURES], F32, name="result")
+                result_sb[step, i] = result
+            nc.vector.scalar_tensor_tensor(
+                out=result_sb[step, i][:, t, cols_of(h)],
+                in0=products[step, i, t, h][:],
+                scalar=2.0,
+                in1=older_of[step][i][:, t, cols_of(h)],
+                op0=MULT,
+                op1=SUBTRACT,
+            )
 
-        older_of = {1: z0_sb, 2: z1_sb}
-        dram_of = {1: z2_dram, 2: z3_dram}
+        def store(step, i, rows, cols=slice(0, FEATURES)):
+            nc.sync.dma_start(out=dram_of[step][i][:, rows, cols], in_=result_sb[step, i][:, rows, cols])
 
-        order = []
-        for g in range(GROUPS + LAG):
-            if g < GROUPS:
-                order.append((1, g))
-            if g >= LAG:
-                order.append((2, g - LAG))
+        order = [(1, 0), (1, 1), (1, 2), (2, 0), (1, 3), (2, 1), (2, 2), (2, 3)]
+        first, last = order[0], order[-1]
+
+        half_by_half = [(t, h) for h in range(HALVES) for t in range(PACK)]
+        row_by_row = [(t, h) for t in range(PACK) for h in range(HALVES)]
+        pair_by_pair = [(t, h) for t0 in (0, 2) for h in range(HALVES) for t in (t0, t0 + 1)]
+
+        def banks_of(unit):
+            if unit == first:
+                return half_by_half
+            if unit == last:
+                return row_by_row
+            return pair_by_pair
+
+        def store_behind(unit, n):
+            step, i = unit
+            t, h = banks_of(unit)[n]
+            if unit == first:
+                if n == 7:
+                    store(step, i, slice(0, PACK))
+            elif unit == last:
+                if t == PACK - 1:
+                    store(step, i, t, cols_of(h))
+                elif h == HALVES - 1:
+                    store(step, i, t)
+            elif n % 4 == 3:
+                store(step, i, slice(t - 1, t + 1))
+
+        def prepare(unit):
+            step, i = unit
+            for h in range(HALVES):
+                quantise(step, i, h)
+            for t, h in banks_of(unit):
+                multiply(step, i, t, h)
 
         regroup_z1(0)
         sort_l_words()
-        quantise(1, 0)
+        quantise(1, 0, 0)
         sort_l_scales()
-        multiply(1, 0)
-        regroup_z1(1)
-        combined = []
+        for t in range(PACK):
+            multiply(1, 0, t, 0)
         for j in range(len(order)):
-            step, g = order[j]
-            if j + 1 < len(order):
-                next_step, next_g = order[j + 1]
-                quantise(next_step, next_g)
-                multiply(next_step, next_g)
-                if next_step == 1 and next_g + 1 < GROUPS:
-                    regroup_z1(next_g + 1)
-            for waiting in combined:
-                regroup_z2(waiting)
-            combined.clear()
-            combine(step, g, older_of[step], dram_of[step])
+            unit = order[j]
+            step, i = unit
+            for n in range(len(banks_of(unit))):
+                t, h = banks_of(unit)[n]
+                if unit == first and n == PACK:
+                    quantise(1, 0, 1)
+                    for t1 in range(PACK):
+                        multiply(1, 0, t1, 1)
+                    regroup_z1(1)
+                combine(step, i, t, h)
+                store_behind(unit, n)
+            if unit != last:
+                following = order[j + 1]
+                prepare(following)
+                if following[0] == 1 and following[1] + 1 < BATCH:
+                    regroup_z1(following[1] + 1)
             if step == 1:
-                combined.append(g)
+                regroup_z2(i)

@@ -190,35 +190,36 @@ def tile_manualchebconv_pb_kernel(tc, z0, z1, L_words, L_scales, out_0, out_1):
             elif n % 4 == 3:
                 store(step, i, slice(t - 1, t + 1))
 
-        def prepare(unit):
-            step, i = unit
-            for h in range(HALVES):
-                quantise(step, i, h)
-            for t, h in banks_of(unit):
-                multiply(step, i, t, h)
+        def quantise_at(following):
+            return (6, 8) if following == (1, 1) else (4, 6)
 
         regroup_z1(0)
         sort_l_words()
         quantise(1, 0, 0)
         sort_l_scales()
-        for t in range(PACK):
-            multiply(1, 0, t, 0)
+        quantise(1, 0, 1)
+        for t, h in banks_of(first):
+            multiply(1, 0, t, h)
+        regroup_z1(1)
         for j in range(len(order)):
             unit = order[j]
             step, i = unit
-            for n in range(len(banks_of(unit))):
-                t, h = banks_of(unit)[n]
-                if unit == first and n == PACK:
-                    quantise(1, 0, 1)
-                    for t1 in range(PACK):
-                        multiply(1, 0, t1, 1)
-                    regroup_z1(1)
-                combine(step, i, t, h)
-                store_behind(unit, n)
-            if unit != last:
-                following = order[j + 1]
-                prepare(following)
-                if following[0] == 1 and following[1] + 1 < BATCH:
-                    regroup_z1(following[1] + 1)
+            following = order[j + 1] if unit != last else None
+            refilled = 0
+            for n in range(len(banks_of(unit)) + 1):
+                if following:
+                    for h in range(HALVES):
+                        if n == quantise_at(following)[h]:
+                            quantise(following[0], following[1], h)
+                    while refilled < n and (following[0], following[1], banks_of(following)[refilled][1]) in quantised:
+                        t, h = banks_of(following)[refilled]
+                        multiply(following[0], following[1], t, h)
+                        refilled += 1
+                if n < len(banks_of(unit)):
+                    t, h = banks_of(unit)[n]
+                    combine(step, i, t, h)
+                    store_behind(unit, n)
+            if following and following[0] == 1 and following[1] + 1 < BATCH:
+                regroup_z1(following[1] + 1)
             if step == 1:
                 regroup_z2(i)

@@ -65,9 +65,11 @@ def tile_manualchebconv_pb_kernel(tc, z0, z1, L_words, L_scales, out_0, out_1):
                 out=l_scales_raw[32 * quadrant : 32 * quadrant + 4, :].bitcast(I32),
                 in_=L_scales[0, 4 * quadrant : 4 * quadrant + 4, :].bitcast(I32),
             )
-        for rows in (slice(0, 2), slice(2, 4)):
-            nc.sync.dma_start(out=z0_sb[0][:, rows, :], in_=z0_dram[0][:, rows, :])
-        for i in range(1, BATCH):
+        nc.sync.dma_start(out=z0_sb[0][:, 0:2, :], in_=z0_dram[0][:, 0:2, :])
+        nc.sync.dma_start(out=z1_sb[1][:], in_=z1_dram[1])
+        nc.sync.dma_start(out=z0_sb[0][:, 2:4, :], in_=z0_dram[0][:, 2:4, :])
+        nc.sync.dma_start(out=z0_sb[1][:], in_=z0_dram[1])
+        for i in range(2, BATCH):
             nc.sync.dma_start(out=z1_sb[i][:], in_=z1_dram[i])
             nc.sync.dma_start(out=z0_sb[i][:], in_=z0_dram[i])
 
@@ -165,33 +167,27 @@ def tile_manualchebconv_pb_kernel(tc, z0, z1, L_words, L_scales, out_0, out_1):
         order = [(1, 0), (1, 1), (1, 2), (2, 0), (1, 3), (2, 1), (2, 2), (2, 3)]
         first, last = order[0], order[-1]
 
-        half_by_half = [(t, h) for h in range(HALVES) for t in range(PACK)]
         row_by_row = [(t, h) for t in range(PACK) for h in range(HALVES)]
         pair_by_pair = [(t, h) for t0 in (0, 2) for h in range(HALVES) for t in (t0, t0 + 1)]
 
         def banks_of(unit):
-            if unit == first:
-                return half_by_half
-            if unit == last:
+            if unit in order[-2:]:
                 return row_by_row
             return pair_by_pair
 
         def store_behind(unit, n):
             step, i = unit
             t, h = banks_of(unit)[n]
-            if unit == first:
-                if n == 7:
-                    store(step, i, slice(0, PACK))
-            elif unit == last:
-                if t == PACK - 1:
-                    store(step, i, t, cols_of(h))
-                elif h == HALVES - 1:
+            if unit == last and t == PACK - 1:
+                store(step, i, t, cols_of(h))
+            elif banks_of(unit) == row_by_row:
+                if h == HALVES - 1:
                     store(step, i, t)
             elif n % 4 == 3:
                 store(step, i, slice(t - 1, t + 1))
 
         def quantise_at(following):
-            return (6, 8) if following == (1, 1) else (4, 6)
+            return (5, 7) if following == (1, 1) else (4, 6)
 
         regroup_z1(0)
         sort_l_words()

@@ -175,19 +175,26 @@ def tile_manualchebconv_pb_kernel(tc, z0, z1, L_words, L_scales, out_0, out_1):
                 return row_by_row
             return pair_by_pair
 
+        def combine_order(unit):
+            filled = banks_of(unit)
+            if unit in order[:2]:
+                return filled
+            return [filled[n] for n in (3, 2, 1, 0, 7, 6, 5, 4)]
+
         def store_behind(unit, n):
             step, i = unit
-            t, h = banks_of(unit)[n]
-            if unit == last and t == PACK - 1:
+            t, h = combine_order(unit)[n]
+            if unit == last and n >= 6:
                 store(step, i, t, cols_of(h))
-            elif banks_of(unit) == row_by_row:
-                if h == HALVES - 1:
+            elif unit in order[-2:]:
+                if n % 2 == 1:
                     store(step, i, t)
             elif n % 4 == 3:
-                store(step, i, slice(t - 1, t + 1))
+                store(step, i, slice(0, 2) if n < 4 else slice(2, 4))
 
         def quantise_at(following):
-            return (5, 7) if following == (1, 1) else (4, 6)
+            late = {order[1]: (5, 7), order[2]: (4, 6)}
+            return late.get(following, (4, 4))
 
         regroup_z1(0)
         sort_l_words()
@@ -207,12 +214,13 @@ def tile_manualchebconv_pb_kernel(tc, z0, z1, L_words, L_scales, out_0, out_1):
                     for h in range(HALVES):
                         if n == quantise_at(following)[h]:
                             quantise(following[0], following[1], h)
-                    while refilled < n and (following[0], following[1], banks_of(following)[refilled][1]) in quantised:
+                    free = n if combine_order(unit) == banks_of(unit) else n // 4 * 4
+                    while refilled < free and (following[0], following[1], banks_of(following)[refilled][1]) in quantised:
                         t, h = banks_of(following)[refilled]
                         multiply(following[0], following[1], t, h)
                         refilled += 1
                 if n < len(banks_of(unit)):
-                    t, h = banks_of(unit)[n]
+                    t, h = combine_order(unit)[n]
                     combine(step, i, t, h)
                     store_behind(unit, n)
             if following and following[0] == 1 and following[1] + 1 < BATCH:

from contextlib import ExitStack

import concourse.mybir as mybir

FP8X4 = mybir.dt.float8_e4m3fn_x4
BF16 = mybir.dt.bfloat16
F32 = mybir.dt.float32
I32 = mybir.dt.int32
U32 = mybir.dt.uint32
U8 = mybir.dt.uint8
MULT = mybir.AluOpType.mult
ADD = mybir.AluOpType.add
SUBTRACT = mybir.AluOpType.subtract

P = 128
PACK = 4
BATCH = 4
NODES = P * PACK
FEATURES = 1024
HALF_F = 512
HALVES = FEATURES // HALF_F
GPSIMD_F = 128

FLOPS = 2 * 2 * BATCH * NODES * NODES * FEATURES


def tile_manualchebconv_pb_kernel(tc, z0, z1, L_words, L_scales, out_0, out_1):
    nc = tc.nc

    def by_item(dram):
        return dram.rearrange("b (p t) f -> b p t f", t=PACK)

    z0_dram, z1_dram, z2_dram, z3_dram = by_item(z0), by_item(z1), by_item(out_0), by_item(out_1)

    def cols_of(h):
        return slice(h * HALF_F, (h + 1) * HALF_F)

    with ExitStack() as ctx:
        consts = ctx.enter_context(tc.tile_pool(name="consts", bufs=1))
        inputs = ctx.enter_context(tc.tile_pool(name="inputs", bufs=1))
        regrouped_z1 = ctx.enter_context(tc.tile_pool(name="regrouped_z1", bufs=1))
        regrouped_z2 = ctx.enter_context(tc.tile_pool(name="regrouped_z2", bufs=4))
        operands = ctx.enter_context(tc.tile_pool(name="operands", bufs=4))
        results = ctx.enter_context(tc.tile_pool(name="results", bufs=7))
        banks = ctx.enter_context(tc.psum_pool(name="banks", bufs=8))
        ctx.enter_context(tc.manual_schedule())

        l_words_raw = consts.tile([P, NODES], U32, name="l_words_raw", align_bytes=64)
        l_scales_raw = consts.tile([P, NODES], U8, name="l_scales_raw", align_bytes=64)
        nc.vector.memset(l_scales_raw[:].bitcast(I32), 0)
        l_words = consts.tile([P, NODES], U32, name="l_words", align_bytes=64)
        l_scales = consts.tile([P, NODES], U8, name="l_scales", align_bytes=64)

        z0_sb, z1_sb = [], []
        for i in range(BATCH):
            z0_item = inputs.tile([P, PACK, FEATURES], BF16, name="z0_item%d" % i)
            z1_item = inputs.tile([P, PACK, FEATURES], BF16, name="z1_item%d" % i)
            z0_sb.append(z0_item)
            z1_sb.append(z1_item)

        nc.sync.dma_start(out=z1_sb[0][:], in_=z1_dram[0])
        nc.sync.dma_start(out=l_words_raw[:].bitcast(I32), in_=L_words[0].rearrange("p n t -> p (n t)").bitcast(I32))
        for quadrant in range(4):
            nc.sync.dma_start(
                out=l_scales_raw[32 * quadrant : 32 * quadrant + 4, :].bitcast(I32),
                in_=L_scales[0, 4 * quadrant : 4 * quadrant + 4, :].bitcast(I32),
            )
        nc.sync.dma_start(out=z0_sb[0][:, 0:2, :], in_=z0_dram[0][:, 0:2, :])
        nc.sync.dma_start(out=z1_sb[1][:], in_=z1_dram[1])
        nc.sync.dma_start(out=z0_sb[0][:, 2:4, :], in_=z0_dram[0][:, 2:4, :])
        nc.sync.dma_start(out=z0_sb[1][:], in_=z0_dram[1])
        for i in range(2, BATCH):
            nc.sync.dma_start(out=z1_sb[i][:], in_=z1_dram[i])
            nc.sync.dma_start(out=z0_sb[i][:], in_=z0_dram[i])

        def sort_l_words():
            nc.vector.tensor_copy(
                out=l_words[:].bitcast(I32).rearrange("p (t m) -> p t m", t=PACK),
                in_=l_words_raw[:].bitcast(I32).rearrange("p (m t) -> p t m", t=PACK),
            )

        def sort_l_scales():
            nc.vector.tensor_copy(
                out=l_scales[:].rearrange("p (t m) -> p t m", t=PACK),
                in_=l_scales_raw[:].rearrange("p (m t) -> p t m", t=PACK),
            )

        grouped = {}
        quantised = {}
        products = {}
        result_sb = {}
        older_of = {1: z0_sb, 2: z1_sb}
        dram_of = {1: z2_dram, 2: z3_dram}

        def regroup(engine_copy, dst, src):
            engine_copy(out=dst, in_=src.rearrange("p t f -> p f t"))

        def regroup_z1(i):
            item = regrouped_z1.tile([P, HALVES, HALF_F, PACK], BF16, name="z1_grouped", align_bytes=64)
            for h in range(HALVES):
                dst = item[:, h, :, :]
                src = z1_sb[i][:, :, cols_of(h)]
                grouped[1, i, h] = dst
                if i == 0 and h == 0:
                    cut = 5 * HALF_F // 8
                    regroup(nc.vector.tensor_copy, dst[:, :cut, :], src[:, :, :cut])
                    regroup(nc.scalar.copy, dst[:, cut:, :], src[:, :, cut:])
                    continue
                for f0 in range(HALF_F // 2, HALF_F, GPSIMD_F):
                    nc.gpsimd.tensor_scalar(
                        out=dst[:, f0 : f0 + GPSIMD_F, :],
                        in0=src[:, :, f0 : f0 + GPSIMD_F].rearrange("p t f -> p f t"),
                        scalar1=1.0,
                        scalar2=0.0,
                        op0=MULT,
                        op1=ADD,
                    )
                regroup(nc.scalar.copy, dst[:, : HALF_F // 2, :], src[:, :, : HALF_F // 2])

        def regroup_z2(i):
            for h in range(HALVES):
                half = regrouped_z2.tile([P, HALF_F, PACK], BF16, name="z2_grouped", align_bytes=64)
                regroup(nc.scalar.copy, half[:], result_sb[1, i][:, :, cols_of(h)])
                grouped[2, i, h] = half[:]

        def quantise(step, i, h):
            codes = operands.tile([P, HALF_F], U32, name="codes%d" % step, align_bytes=64)
            scales = operands.tile([P, HALF_F], U8, name="scales%d" % step, align_bytes=64)
            nc.vector.quantize_mx(
                out=codes[:].bitcast(FP8X4),
                scales=scales[:],
                in_=grouped[step, i, h].rearrange("p f t -> p (f t)"),
            )
            quantised[step, i, h] = (codes, scales)

        def multiply(step, i, t, h):
            codes, scales = quantised[step, i, h]
            sorted_cols = slice(t * P, (t + 1) * P)
            bank = banks.tile([P, HALF_F], F32, name="bank")
            nc.tensor.matmul_mx(
                out=bank[:],
                lhsT=l_words[:, sorted_cols].bitcast(FP8X4),
                lhsT_scale=l_scales[:, sorted_cols],
                rhs=codes[:].bitcast(FP8X4),
                rhs_scale=scales[:],
                start=True,
                stop=True,
            )
            products[step, i, t, h] = bank

        def combine(step, i, t, h):
            if (step, i) not in result_sb:
                result = results.tile([P, PACK, FEATURES], F32, name="result")
                result_sb[step, i] = result
            nc.vector.scalar_tensor_tensor(
                out=result_sb[step, i][:, t, cols_of(h)],
                in0=products[step, i, t, h][:],
                scalar=2.0,
                in1=older_of[step][i][:, t, cols_of(h)],
                op0=MULT,
                op1=SUBTRACT,
            )

        def store(step, i, rows, cols=slice(0, FEATURES)):
            nc.sync.dma_start(out=dram_of[step][i][:, rows, cols], in_=result_sb[step, i][:, rows, cols])

        order = [(1, 0), (1, 1), (1, 2), (2, 0), (1, 3), (2, 1), (2, 2), (2, 3)]
        first, last = order[0], order[-1]

        row_by_row = [(t, h) for t in range(PACK) for h in range(HALVES)]
        pair_by_pair = [(t, h) for t0 in (0, 2) for h in range(HALVES) for t in (t0, t0 + 1)]

        def banks_of(unit):
            if unit in order[-2:]:
                return row_by_row
            return pair_by_pair

        def combine_order(unit):
            filled = banks_of(unit)
            if unit in order[:2]:
                return filled
            return [filled[n] for n in (3, 2, 1, 0, 7, 6, 5, 4)]

        def store_behind(unit, n):
            step, i = unit
            t, h = combine_order(unit)[n]
            if unit == last and n >= 6:
                store(step, i, t, cols_of(h))
            elif unit in order[-2:]:
                if n % 2 == 1:
                    store(step, i, t)
            elif n % 4 == 3:
                store(step, i, slice(0, 2) if n < 4 else slice(2, 4))

        def quantise_at(following):
            late = {order[1]: (5, 7), order[2]: (4, 6)}
            return late.get(following, (4, 4))

        regroup_z1(0)
        sort_l_words()
        quantise(1, 0, 0)
        sort_l_scales()
        quantise(1, 0, 1)
        for t, h in banks_of(first):
            multiply(1, 0, t, h)
        regroup_z1(1)
        for j in range(len(order)):
            unit = order[j]
            step, i = unit
            following = order[j + 1] if unit != last else None
            refilled = 0
            for n in range(len(banks_of(unit)) + 1):
                if following:
                    for h in range(HALVES):
                        if n == quantise_at(following)[h]:
                            quantise(following[0], following[1], h)
                    free = n if combine_order(unit) == banks_of(unit) else n // 4 * 4
                    while refilled < free and (following[0], following[1], banks_of(following)[refilled][1]) in quantised:
                        t, h = banks_of(following)[refilled]
                        multiply(following[0], following[1], t, h)
                        refilled += 1
                if n < len(banks_of(unit)):
                    t, h = combine_order(unit)[n]
                    combine(step, i, t, h)
                    store_behind(unit, n)
            if following and following[0] == 1 and following[1] + 1 < BATCH:
                regroup_z1(following[1] + 1)
            if step == 1:
                regroup_z2(i)
